import numpy as np
import ml_dtypes


def mxq(x, axis, fmt="e4m3"):
    dtype, down = {"e4m3": (ml_dtypes.float8_e4m3fn, 7), "e5m2": (ml_dtypes.float8_e5m2, 14)}[fmt]
    v = np.moveaxis(np.asarray(x, np.float32).astype(ml_dtypes.bfloat16).astype(np.float64), axis, -1)
    blocks = v.reshape(v.shape[:-1] + (-1, 32))
    amax = np.abs(blocks).max(-1, keepdims=True)
    byte = np.maximum(np.where(amax > 0, np.frexp(amax)[1] - 1 + 127, 0) - down, 1)
    scale = np.exp2(byte - 127.0)
    codes = (blocks / scale).astype(np.float32).astype(dtype).astype(np.float64)
    return np.moveaxis((codes * scale).reshape(v.shape), -1, axis)


WIDE = False


def mx_kscale(k):
    if not WIDE:
        return np.ones(k)
    levels = np.array([10, -10, 5, -5, 0])
    a = np.random.permutation(np.resize(levels, k // 512 * 4)).reshape(k // 512, 4)
    idx = np.arange(k)
    return np.exp2(a[idx // 512, idx % 128 // 32])


BF16 = ml_dtypes.bfloat16


def bf(x):
    return np.asarray(x, np.float32).astype(BF16)


def f64(x):
    return np.asarray(x).astype(np.float64)


E2M1 = np.array([0.0, 0.5, 1.0, 1.5, 2.0, 3.0, 4.0, 6.0, -0.0, -0.5, -1.0, -1.5, -2.0, -3.0, -4.0, -6.0])


def pack_weight(w, fmt):
    k, n = w.shape
    w = f64(bf(w)).reshape(k // 32, 32, n)
    amax = np.abs(w).max(1)
    if fmt == "e4m3":
        byte = np.frexp(amax)[1] - 1 + 127 - 7
    else:
        mant, ex = np.frexp(amax / 6.0)
        byte = np.where(mant > 0.5, ex, ex - 1) + 127
    byte = np.clip(np.where(amax > 0, byte, 1), 1, 254)
    scaled = (w * np.exp2(127.0 - byte)[:, None, :]).reshape(k, n).astype(np.float32)
    by_word = np.ascontiguousarray(scaled.reshape(k // 512, 128, 4, n).transpose(0, 1, 3, 2))
    if fmt == "e4m3":
        words = by_word.astype(ml_dtypes.float8_e4m3fn).view(np.uint8)
    else:
        c = by_word.astype(ml_dtypes.float4_e2m1fn).view(np.uint8) & 0xF
        words = c[..., 0::2] | (c[..., 1::2] << 4)
    return np.ascontiguousarray(words), np.ascontiguousarray(byte.astype(np.uint8).reshape(k // 512, 16, n))


def unpack_weight(words, scales, fmt):
    g, p, n, _ = words.shape
    if fmt == "e4m3":
        vals = np.ascontiguousarray(words).view(ml_dtypes.float8_e4m3fn).astype(np.float64)
    else:
        nib = np.empty((g, p, n, 4), np.uint8)
        nib[..., 0::2] = words & 0xF
        nib[..., 1::2] = words >> 4
        vals = E2M1[nib]
    vals = vals * np.repeat(np.exp2(scales.astype(np.float64) - 127.0), 8, axis=1)[..., None]
    return vals.transpose(0, 1, 3, 2).reshape(g * 512, n)

def pack4(w):
    words, scales = pack_weight(w, "e2m1")
    return words.reshape(words.shape[0], 128, -1), scales


def unpack4(words, scales):
    return unpack_weight(words.reshape(words.shape[0], 128, -1, 2), scales, "e2m1")


B, S, HID, H, D = 4, 2048, 512, 2, 64
QKV = 3 * H * D


def rotate_half(x):
    x1, x2 = x[..., : x.shape[-1] // 2], x[..., x.shape[-1] // 2 :]
    return np.concatenate((-x2, x1), axis=-1)


def setup_inputs():
    s = mx_kscale(HID)
    hidden_states = bf(np.random.standard_normal((B, S, HID)) * s)
    cos = bf(np.random.uniform(size=(S, D)))
    sin = bf(np.random.uniform(size=(S, D)))
    words, scales = pack4(np.random.standard_normal((HID, QKV)) * 2.0 / np.sqrt(HID) / s[:, None])
    return {"hidden_states": hidden_states,
            "cos": cos,
            "sin": sin,
            "w_qkv_words": words,
            "w_qkv_scales": scales}


def reference(hidden_states, cos, sin, w_qkv_words, w_qkv_scales):
    qkv = mxq(f64(hidden_states), 2, "e4m3") @ unpack4(w_qkv_words, w_qkv_scales)
    qkv = qkv.reshape(B, S, 3 * H, D)
    q, k, v = qkv[:, :, :H], qkv[:, :, H:2 * H], qkv[:, :, 2 * H:]
    c = f64(cos)[:, None, :]
    sn = f64(sin)[:, None, :]
    q_rot = q * c + rotate_half(q) * sn
    k_rot = k * c + rotate_half(k) * sn
    return q_rot, k_rot, v

@@ -1,0 +1,266 @@
+from contextlib import ExitStack
+
+import concourse.mybir as mybir
+from concourse.masks import make_identity
+
+F32 = mybir.dt.float32
+BF16 = mybir.dt.bfloat16
+I32 = mybir.dt.int32
+U32 = mybir.dt.uint32
+U8 = mybir.dt.uint8
+FP8X4 = mybir.dt.float8_e4m3fn_x4
+FP4X4 = mybir.dt.float4_e2m1fn_x4
+MULT = mybir.AluOpType.mult
+ADD = mybir.AluOpType.add
+
+P = 128
+BATCH, SEQ, HID = 4, 2048, 512
+HEAD = 64
+HALF = HEAD // 2
+QK_HEADS = 4
+QK = QK_HEADS * HEAD
+V = 2 * HEAD
+ROWS = SEQ // P
+TILES = 4
+GROUP_TILES = [2, 2] + [TILES] * (BATCH * ROWS // TILES - 1)
+GROUPS = len(GROUP_TILES)
+
+FLOPS = 2 * BATCH * SEQ * HID * (QK + V)
+
+
+def tile_attention_pa_t_kernel(
+    tc, hidden_states, cos, sin, w_qkv_words, w_qkv_scales, out_0, out_1, out_2
+):
+    nc = tc.nc
+    x_hbm = hidden_states.rearrange("b (p j) k -> b p j k", j=ROWS)
+    q_hbm = out_0.rearrange("b (p j) h d -> b p j (h d)", j=ROWS)
+    k_hbm = out_1.rearrange("b (p j) h d -> b p j (h d)", j=ROWS)
+    v_hbm = out_2.rearrange("b (p j) h d -> b p j (h d)", j=ROWS)
+
+    with ExitStack() as stack:
+        consts = stack.enter_context(tc.tile_pool(name="consts", bufs=1))
+        x_pool = stack.enter_context(tc.tile_pool(name="x", bufs=GROUPS))
+        grouped_pool = stack.enter_context(tc.tile_pool(name="grouped", bufs=5))
+        mx_pool = stack.enter_context(tc.tile_pool(name="mx", bufs=6))
+        product_pool = stack.enter_context(tc.tile_pool(name="products", bufs=3))
+        out_pool = stack.enter_context(tc.tile_pool(name="outputs", bufs=6))
+        xt_psum = stack.enter_context(tc.psum_pool(name="xt", bufs=2))
+        qkv_psum = stack.enter_context(tc.psum_pool(name="qkv", bufs=2))
+        stack.enter_context(tc.manual_schedule())
+
+        x_tiles, xt_tiles, grouped_tiles, code_tiles, scale_tiles = {}, {}, {}, {}, {}
+        qk_banks, v_banks = {}, {}
+
+        def where(g):
+            first = sum(GROUP_TILES[:g])
+            return first // ROWS, first % ROWS, GROUP_TILES[g]
+
+        def load(g):
+            b, j0, n = where(g)
+            x_tile = x_pool.tile([P, n, HID], BF16)
+            nc.sync.dma_start(out=x_tile[:], in_=x_hbm[b, :, j0 : j0 + n, :])
+            x_tiles[g] = x_tile
+
+        identity = consts.tile([P, P], F32)
+        make_identity(nc, identity[:])
+
+        w_words = consts.tile([P, 2 * (QK + V)], U8, align_bytes=64)
+        w_scales = consts.tile([P, QK + V], U8, align_bytes=64)
+        nc.vector.memset(w_scales[:].bitcast(I32), 0)
+        tables = consts.tile([P, 2, ROWS, HEAD], BF16)
+
+        load(0)
+        nc.sync.dma_start(out=w_words[:].bitcast(I32), in_=w_qkv_words[0].bitcast(I32))
+        for quadrant in range(4):
+            nc.sync.dma_start(
+                out=w_scales[32 * quadrant : 32 * quadrant + 4, :].bitcast(I32),
+                in_=w_qkv_scales[0, 4 * quadrant : 4 * quadrant + 4, :].bitcast(I32),
+            )
+        load(1)
+        nc.sync.dma_start(out=tables[:, 0, :, :], in_=cos.rearrange("(p j) d -> p j d", j=ROWS))
+        nc.sync.dma_start(out=tables[:, 1, :, :], in_=sin.rearrange("(p j) d -> p j d", j=ROWS))
+        for g in range(2, GROUPS):
+            load(g)
+
+        nc.vector.tensor_scalar(
+            out=tables[:, 1, :, 0:HALF],
+            in0=tables[:, 1, :, 0:HALF],
+            scalar1=-1.0,
+            scalar2=None,
+            op0=MULT,
+        )
+
+        def transpose(g):
+            x_words = x_tiles[g][:].bitcast(F32)
+            xt_tiles[g] = []
+            for pair in range(GROUP_TILES[g] // 2):
+                x_transposed = xt_psum.tile([P, 2, 2, P], F32)
+                for t in range(2):
+                    for u in range(2):
+                        nc.tensor.transpose(
+                            x_transposed[:, t, u, :],
+                            x_words[:, 2 * pair + t, u : HID // 2 : 2],
+                            identity[:],
+                        )
+                xt_tiles[g].append(x_transposed)
+
+        def regroup(g):
+            n = GROUP_TILES[g]
+            grouped = grouped_pool.tile([P, n * P * 4], BF16, align_bytes=64)
+            grouped_words = grouped[:].bitcast(F32).rearrange("p (t r u) -> p t r u", t=n, u=2)
+            for pair in range(n // 2):
+                nc.scalar.copy(
+                    out=grouped_words[:, 2 * pair : 2 * pair + 2, :, :],
+                    in_=xt_tiles[g][pair][:].rearrange("p t u r -> p t r u"),
+                )
+            grouped_tiles[g] = grouped
+
+        def quantise(g):
+            codes = mx_pool.tile([P, GROUP_TILES[g] * P], U32, align_bytes=64)
+            scales = mx_pool.tile([P, GROUP_TILES[g] * P], U8, align_bytes=64)
+            nc.vector.quantize_mx(
+                out=codes[:].bitcast(FP8X4), scales=scales[:], in_=grouped_tiles[g][:]
+            )
+            code_tiles[g], scale_tiles[g] = codes, scales
+
+        def project(g):
+            q_bank = qkv_psum.tile([P, GROUP_TILES[g], V], F32)
+            k_bank = qkv_psum.tile([P, GROUP_TILES[g], V], F32)
+            v_bank = qkv_psum.tile([P, GROUP_TILES[g], V], F32)
+            for n, bank in enumerate((q_bank, k_bank, v_bank)):
+                for t in range(GROUP_TILES[g]):
+                    tokens = slice(P * t, P * (t + 1))
+                    nc.tensor.matmul_mx(
+                        out=bank[:, t, :],
+                        lhsT=code_tiles[g][:, tokens].bitcast(FP8X4),
+                        lhsT_scale=scale_tiles[g][:, tokens],
+                        rhs=w_words[:, 2 * V * n : 2 * V * (n + 1)].bitcast(FP4X4),
+                        rhs_scale=w_scales[:, V * n : V * (n + 1)],
+                        start=True,
+                        stop=True,
+                    )
+            qk_banks[g] = (q_bank, k_bank)
+            v_banks[g] = v_bank
+
+        def store_v(g):
+            b, j0, n = where(g)
+            v_out = out_pool.tile([P, n, V], F32)
+            nc.scalar.copy(out=v_out[:], in_=v_banks[g][:])
+            nc.sync.dma_start(out=v_hbm[b, :, j0 : j0 + n, :], in_=v_out[:])
+
+        def rotate(products, first, g, a, c, t0=0, t1=None):
+            b, j0, n = where(g)
+            t1 = n if t1 is None else t1
+            first, j0, n = first + t0, j0 + t0, t1 - t0
+            halves = qk_banks[g][a][:, t0:t1, :].rearrange(
+                "p t (g two w) -> p t g two w", two=2, w=HALF
+            )
+            nc.vector.tensor_tensor(
+                out=products[:, c, a, first : first + n, :].rearrange(
+                    "p t (g two w) -> p t g two w", two=2, w=HALF
+                ),
+                in0=halves if c == 0 else halves[:, :, :, ::-1, :],
+                in1=tables[:, c, j0 : j0 + n, :]
+                .rearrange("p t (two w) -> p t two w", two=2)
+                .unsqueeze(2)
+                .to_broadcast([P, n, V // HEAD, 2, HALF]),
+                op=MULT,
+            )
+
+        def add(engine, products, qk_out, region):
+            a0, a1, first, last = region
+            engine.tensor_tensor(
+                out=qk_out[:, a0:a1, first:last, :],
+                in0=products[:, 0, a0:a1, first:last, :],
+                in1=products[:, 1, a0:a1, first:last, :],
+                op=ADD,
+            )
+
+        def store_qk(groups, qk_out, first, last):
+            b, j0, n = where(groups[0])
+            rows = slice(j0 + first, j0 + last)
+            nc.sync.dma_start(out=q_hbm[b, :, rows, :], in_=qk_out[:, 0, first:last, :])
+            nc.sync.dma_start(out=k_hbm[b, :, rows, :], in_=qk_out[:, 1, first:last, :])
+
+        rounds = [[0], [1], [2]] + [[g, g + 1] for g in range(3, GROUPS, 2)]
+        ahead = [[1], [2], [3, 4], [5, 6, 7]] + [
+            [g for g in (groups[-1] + 2, groups[-1] + 3) if g < GROUPS] for groups in rounds[4:]
+        ]
+        rotated, quantised, projected = [], [], []
+
+        def project_what_can_be():
+            while (
+                len(projected) < GROUPS
+                and len(projected) in quantised
+                and (len(projected) < 2 or len(projected) - 2 in rotated)
+            ):
+                project(len(projected))
+                store_v(len(projected))
+                projected.append(len(projected))
+
+        for g in [0] + ahead[0]:
+            transpose(g)
+            regroup(g)
+        quantise(0)
+        quantised.append(0)
+        project_what_can_be()
+        waiting = None
+        for r, groups in enumerate(rounds):
+            last_round = r + 1 == len(rounds)
+            count = sum(GROUP_TILES[g] for g in groups)
+            if last_round:
+                before, after = [(0, 2, 0, TILES)], [(0, 2, TILES, count - 2), (0, 2, count - 2, count)]
+            elif sum(GROUP_TILES[g] for g in rounds[r + 1]) > count:
+                before, after = [], [(0, 2, 0, count)]
+            elif len(groups) == 1:
+                before, after = [(0, 1, 0, 1)], [(0, 1, 1, count), (1, 2, 0, count)]
+            elif r + 2 == len(rounds):
+                before, after = [(0, 2, 0, 1)], [(0, 2, 1, TILES), (0, 2, TILES, count)]
+            else:
+                before, after = [(0, 2, 0, 1)], [(0, 2, 1, count)]
+            to_transpose = ahead[r + 1] if not last_round else []
+            products = product_pool.tile([P, 2, 2, count, 2 * HEAD], F32)
+            qk_out = out_pool.tile([P, 2, count, 2 * HEAD], F32)
+            slots = [
+                (sum(GROUP_TILES[m] for m in groups[:n]), g, a, c)
+                for n, g in enumerate(groups)
+                for a in range(2)
+                for c in range(2)
+            ]
+            late = 2 if last_round else 1
+            for first, g, a, c in slots[:-late]:
+                rotate(products, first, g, a, c)
+                if a == 1 and c == 1:
+                    rotated.append(g)
+                    project_what_can_be()
+            if not last_round:
+                first, g, a, c = slots[-1]
+                rotate(products, first, g, a, c, 0, GROUP_TILES[g] - 1)
+            if waiting is not None:
+                for first in range(0, waiting[2], TILES):
+                    store_qk(waiting[0], waiting[1], first, min(first + TILES, waiting[2]))
+            for g in to_transpose[:1]:
+                transpose(g)
+                regroup(g)
+            for region in before:
+                add(nc.vector, products, qk_out, region)
+                if last_round:
+                    store_qk(groups, qk_out, region[2], region[3])
+            for g in ahead[r]:
+                quantise(g)
+                quantised.append(g)
+            for first, g, a, c in slots[-late:]:
+                rotate(products, first, g, a, c, 0 if last_round else GROUP_TILES[g] - 1)
+            rotated.append(g)
+            project_what_can_be()
+            for g in to_transpose[1:]:
+                transpose(g)
+                regroup(g)
+            if not last_round:
+                for region in after:
+                    add(nc.gpsimd, products, qk_out, region)
+                waiting = (groups, qk_out, count)
+            else:
+                for region in after:
+                    add(nc.vector, products, qk_out, region)
+                    store_qk(groups, qk_out, region[2], region[3])

@@ -82,13 +82,6 @@ def tile_attention_pa_t_kernel(
         for g in range(2, GROUPS):
             load(g)
 
-        nc.vector.tensor_scalar(
-            out=tables[:, 1, :, 0:HALF],
-            in0=tables[:, 1, :, 0:HALF],
-            scalar1=-1.0,
-            scalar2=None,
-            op0=MULT,
-        )
 
         def transpose(g):
             x_words = x_tiles[g][:].bitcast(F32)
@@ -204,6 +197,13 @@ def tile_attention_pa_t_kernel(
         quantise(0)
         quantised.append(0)
         project_what_can_be()
+        nc.vector.tensor_scalar(
+            out=tables[:, 1, :, 0:HALF],
+            in0=tables[:, 1, :, 0:HALF],
+            scalar1=-1.0,
+            scalar2=None,
+            op0=MULT,
+        )
         waiting = None
         for r, groups in enumerate(rounds):
             last_round = r + 1 == len(rounds)

@@ -22,8 +22,19 @@ QK = QK_HEADS * HEAD
 V = 2 * HEAD
 ROWS = SEQ // P
 TILES = 4
-GROUP_TILES = [2, 2] + [TILES] * (BATCH * ROWS // TILES - 1)
+PAIR = 2
+GROUP_TILES = [2, 2, 2, 2] + [TILES] * (BATCH * ROWS // TILES - 2)
 GROUPS = len(GROUP_TILES)
+
+STRETCHES = [[0], [1], [2], [3], [4], [5, 6], [7, 8], [9, 10, 11], [12, 13, 14], [15, 16, 17]]
+LEAD = [3, 3, 3, 4, 4, 4, 4, 4, 4, 4]
+OWN = [[], [], [], [], [], [2], [], [4], [4], [2]]
+VECTOR = [1, 1, 1, 0, 0, 0, 0, 1, 1, 0]
+
+QK_BANKS = 4
+PREPARED = 6
+BATCH_TILES = 16
+LOADED_AHEAD = 8
 
 FLOPS = 2 * BATCH * SEQ * HID * (QK + V)
 
@@ -39,13 +50,15 @@ def tile_attention_pa_t_kernel(
 
     with ExitStack() as stack:
         consts = stack.enter_context(tc.tile_pool(name="consts", bufs=1))
-        x_pool = stack.enter_context(tc.tile_pool(name="x", bufs=GROUPS))
-        grouped_pool = stack.enter_context(tc.tile_pool(name="grouped", bufs=5))
-        mx_pool = stack.enter_context(tc.tile_pool(name="mx", bufs=6))
-        product_pool = stack.enter_context(tc.tile_pool(name="products", bufs=3))
-        out_pool = stack.enter_context(tc.tile_pool(name="outputs", bufs=6))
+        x_pool = stack.enter_context(tc.tile_pool(name="x", bufs=LOADED_AHEAD))
+        grouped_pool = stack.enter_context(tc.tile_pool(name="grouped", bufs=PREPARED))
+        mx_pool = stack.enter_context(tc.tile_pool(name="mx", bufs=7))
+        product_pool = stack.enter_context(tc.tile_pool(name="products", bufs=2))
+        qk_pool = stack.enter_context(tc.tile_pool(name="qk", bufs=4))
+        v_pool = stack.enter_context(tc.tile_pool(name="v", bufs=8))
         xt_psum = stack.enter_context(tc.psum_pool(name="xt", bufs=2))
-        qkv_psum = stack.enter_context(tc.psum_pool(name="qkv", bufs=2))
+        qk_psum = stack.enter_context(tc.psum_pool(name="qk_sums", bufs=QK_BANKS))
+        v_psum = stack.enter_context(tc.psum_pool(name="v_sums", bufs=2))
         stack.enter_context(tc.manual_schedule())
 
         x_tiles, xt_tiles, grouped_tiles, code_tiles, scale_tiles = {}, {}, {}, {}, {}
@@ -78,21 +91,21 @@ def tile_attention_pa_t_kernel(
             )
         load(1)
         nc.sync.dma_start(out=tables[:, 0, :, :], in_=cos.rearrange("(p j) d -> p j d", j=ROWS))
+        load(2)
         nc.sync.dma_start(out=tables[:, 1, :, :], in_=sin.rearrange("(p j) d -> p j d", j=ROWS))
-        for g in range(2, GROUPS):
+        for g in range(3, LOADED_AHEAD):
             load(g)
-
 
         def transpose(g):
             x_words = x_tiles[g][:].bitcast(F32)
             xt_tiles[g] = []
-            for pair in range(GROUP_TILES[g] // 2):
-                x_transposed = xt_psum.tile([P, 2, 2, P], F32)
-                for t in range(2):
+            for pair in range(GROUP_TILES[g] // PAIR):
+                x_transposed = xt_psum.tile([P, PAIR, 2, P], F32)
+                for t in range(PAIR):
                     for u in range(2):
                         nc.tensor.transpose(
                             x_transposed[:, t, u, :],
-                            x_words[:, 2 * pair + t, u : HID // 2 : 2],
+                            x_words[:, PAIR * pair + t, u : HID // 2 : 2],
                             identity[:],
                         )
                 xt_tiles[g].append(x_transposed)
@@ -101,9 +114,9 @@ def tile_attention_pa_t_kernel(
             n = GROUP_TILES[g]
             grouped = grouped_pool.tile([P, n * P * 4], BF16, align_bytes=64)
             grouped_words = grouped[:].bitcast(F32).rearrange("p (t r u) -> p t r u", t=n, u=2)
-            for pair in range(n // 2):
+            for pair in range(n // PAIR):
                 nc.scalar.copy(
-                    out=grouped_words[:, 2 * pair : 2 * pair + 2, :, :],
+                    out=grouped_words[:, PAIR * pair : PAIR * (pair + 1), :, :],
                     in_=xt_tiles[g][pair][:].rearrange("p t u r -> p t r u"),
                 )
             grouped_tiles[g] = grouped
@@ -116,151 +129,167 @@ def tile_attention_pa_t_kernel(
             )
             code_tiles[g], scale_tiles[g] = codes, scales
 
+        def multiply(bank_columns, g, t, first, last):
+            tokens = slice(P * t, P * (t + 1))
+            nc.tensor.matmul_mx(
+                out=bank_columns,
+                lhsT=code_tiles[g][:, tokens].bitcast(FP8X4),
+                lhsT_scale=scale_tiles[g][:, tokens],
+                rhs=w_words[:, 2 * first : 2 * last].bitcast(FP4X4),
+                rhs_scale=w_scales[:, first:last],
+                start=True,
+                stop=True,
+            )
+
         def project(g):
-            q_bank = qkv_psum.tile([P, GROUP_TILES[g], V], F32)
-            k_bank = qkv_psum.tile([P, GROUP_TILES[g], V], F32)
-            v_bank = qkv_psum.tile([P, GROUP_TILES[g], V], F32)
-            for n, bank in enumerate((q_bank, k_bank, v_bank)):
-                for t in range(GROUP_TILES[g]):
-                    tokens = slice(P * t, P * (t + 1))
-                    nc.tensor.matmul_mx(
-                        out=bank[:, t, :],
-                        lhsT=code_tiles[g][:, tokens].bitcast(FP8X4),
-                        lhsT_scale=scale_tiles[g][:, tokens],
-                        rhs=w_words[:, 2 * V * n : 2 * V * (n + 1)].bitcast(FP4X4),
-                        rhs_scale=w_scales[:, V * n : V * (n + 1)],
-                        start=True,
-                        stop=True,
-                    )
-            qk_banks[g] = (q_bank, k_bank)
+            qk_banks[g] = []
+            for pair in range(GROUP_TILES[g] // PAIR):
+                qk_bank = qk_psum.tile([P, PAIR, QK], F32)
+                for t in range(PAIR):
+                    multiply(qk_bank[:, t, :], g, PAIR * pair + t, 0, QK)
+                qk_banks[g].append(qk_bank)
+            v_bank = v_psum.tile([P, GROUP_TILES[g], V], F32)
+            for t in range(GROUP_TILES[g]):
+                multiply(v_bank[:, t, :], g, t, QK, QK + V)
             v_banks[g] = v_bank
 
         def store_v(g):
             b, j0, n = where(g)
-            v_out = out_pool.tile([P, n, V], F32)
+            v_out = v_pool.tile([P, n, V], F32)
             nc.scalar.copy(out=v_out[:], in_=v_banks[g][:])
             nc.sync.dma_start(out=v_hbm[b, :, j0 : j0 + n, :], in_=v_out[:])
 
-        def rotate(products, first, g, a, c, t0=0, t1=None):
-            b, j0, n = where(g)
-            t1 = n if t1 is None else t1
-            first, j0, n = first + t0, j0 + t0, t1 - t0
-            halves = qk_banks[g][a][:, t0:t1, :].rearrange(
+        def rotate(products, first, g, pair, c, t0=0, t1=PAIR):
+            j0, first, n = where(g)[1] + PAIR * pair + t0, first + t0, t1 - t0
+            halves = qk_banks[g][pair][:, t0:t1, :].rearrange(
                 "p t (g two w) -> p t g two w", two=2, w=HALF
             )
             nc.vector.tensor_tensor(
-                out=products[:, c, a, first : first + n, :].rearrange(
+                out=products[:, c, first : first + n, :].rearrange(
                     "p t (g two w) -> p t g two w", two=2, w=HALF
                 ),
                 in0=halves if c == 0 else halves[:, :, :, ::-1, :],
                 in1=tables[:, c, j0 : j0 + n, :]
                 .rearrange("p t (two w) -> p t two w", two=2)
                 .unsqueeze(2)
-                .to_broadcast([P, n, V // HEAD, 2, HALF]),
+                .to_broadcast([P, n, QK_HEADS, 2, HALF]),
                 op=MULT,
             )
 
-        def add(engine, products, qk_out, region):
-            a0, a1, first, last = region
+        def add(engine, products, qk_out, first, last):
             engine.tensor_tensor(
-                out=qk_out[:, a0:a1, first:last, :],
-                in0=products[:, 0, a0:a1, first:last, :],
-                in1=products[:, 1, a0:a1, first:last, :],
+                out=qk_out[:, :, first:last, :].rearrange("p a t w -> p t a w"),
+                in0=products[:, 0, first:last, :].rearrange("p t (a w) -> p t a w", a=2),
+                in1=products[:, 1, first:last, :].rearrange("p t (a w) -> p t a w", a=2),
                 op=ADD,
             )
 
         def store_qk(groups, qk_out, first, last):
-            b, j0, n = where(groups[0])
-            rows = slice(j0 + first, j0 + last)
-            nc.sync.dma_start(out=q_hbm[b, :, rows, :], in_=qk_out[:, 0, first:last, :])
-            nc.sync.dma_start(out=k_hbm[b, :, rows, :], in_=qk_out[:, 1, first:last, :])
+            start = sum(GROUP_TILES[: groups[0]])
+            while first < last:
+                b, j0 = (start + first) // ROWS, (start + first) % ROWS
+                n = min(last - first, ROWS - j0)
+                for a, hbm in enumerate((q_hbm, k_hbm)):
+                    nc.sync.dma_start(
+                        out=hbm[b, :, j0 : j0 + n, :], in_=qk_out[:, a, first : first + n, :]
+                    )
+                first += n
 
-        rounds = [[0], [1], [2]] + [[g, g + 1] for g in range(3, GROUPS, 2)]
-        ahead = [[1], [2], [3, 4], [5, 6, 7]] + [
-            [g for g in (groups[-1] + 2, groups[-1] + 3) if g < GROUPS] for groups in rounds[4:]
-        ]
-        rotated, quantised, projected = [], [], []
+        rotated, quantised, projected, transposed = [], [], [], []
+
+        def flip_sign():
+            nc.vector.tensor_scalar(
+                out=tables[:, 1, :, 0:HALF],
+                in0=tables[:, 1, :, 0:HALF],
+                scalar1=-1.0,
+                scalar2=None,
+                op0=MULT,
+            )
+
+        def tiles_of(groups):
+            return sum(GROUP_TILES[g] for g in groups)
 
         def project_what_can_be():
             while (
-                len(projected) < GROUPS
-                and len(projected) in quantised
-                and (len(projected) < 2 or len(projected) - 2 in rotated)
+                len(projected) < len(quantised)
+                and tiles_of(projected + [len(projected)]) - tiles_of(rotated) <= PAIR * QK_BANKS
             ):
                 project(len(projected))
                 store_v(len(projected))
                 projected.append(len(projected))
 
-        for g in [0] + ahead[0]:
-            transpose(g)
-            regroup(g)
-        quantise(0)
-        quantised.append(0)
+        def prepare_to(g):
+            while len(transposed) <= min(g, GROUPS - 1):
+                transpose(len(transposed))
+                regroup(len(transposed))
+                if len(transposed) + LOADED_AHEAD < GROUPS:
+                    load(len(transposed) + LOADED_AHEAD)
+                transposed.append(len(transposed))
+
+        def quantise_to(g):
+            while len(quantised) <= g:
+                quantise(len(quantised))
+                quantised.append(len(quantised))
+
+        def due_behind(s):
+            return STRETCHES[s + 2][0] if s + 2 < len(STRETCHES) else GROUPS - 1
+
+        prepare_to(1)
+        quantise_to(0)
         project_what_can_be()
-        nc.vector.tensor_scalar(
-            out=tables[:, 1, :, 0:HALF],
-            in0=tables[:, 1, :, 0:HALF],
-            scalar1=-1.0,
-            scalar2=None,
-            op0=MULT,
-        )
+        prepare_to(2)
+        quantise_to(1)
+        project_what_can_be()
         waiting = None
-        for r, groups in enumerate(rounds):
-            last_round = r + 1 == len(rounds)
-            count = sum(GROUP_TILES[g] for g in groups)
-            if last_round:
-                before, after = [(0, 2, 0, TILES)], [(0, 2, TILES, count - 2), (0, 2, count - 2, count)]
-            elif sum(GROUP_TILES[g] for g in rounds[r + 1]) > count:
-                before, after = [], [(0, 2, 0, count)]
-            elif len(groups) == 1:
-                before, after = [(0, 1, 0, 1)], [(0, 1, 1, count), (1, 2, 0, count)]
-            elif r + 2 == len(rounds):
-                before, after = [(0, 2, 0, 1)], [(0, 2, 1, TILES), (0, 2, TILES, count)]
-            else:
-                before, after = [(0, 2, 0, 1)], [(0, 2, 1, count)]
-            to_transpose = ahead[r + 1] if not last_round else []
-            products = product_pool.tile([P, 2, 2, count, 2 * HEAD], F32)
-            qk_out = out_pool.tile([P, 2, count, 2 * HEAD], F32)
-            slots = [
-                (sum(GROUP_TILES[m] for m in groups[:n]), g, a, c)
-                for n, g in enumerate(groups)
-                for a in range(2)
-                for c in range(2)
-            ]
-            late = 2 if last_round else 1
-            for first, g, a, c in slots[:-late]:
-                rotate(products, first, g, a, c)
-                if a == 1 and c == 1:
+        for s, groups in enumerate(STRETCHES):
+            last_stretch = s + 1 == len(STRETCHES)
+            count = tiles_of(groups)
+            products = product_pool.tile([P, 2, count, QK], F32)
+            qk_out = qk_pool.tile([P, 2, count, V], F32)
+            stores, added = [], 0
+            if waiting is not None:
+                for hi in range(waiting[4], waiting[3], -BATCH_TILES):
+                    lo = max(hi - BATCH_TILES, waiting[3])
+                    add(nc.gpsimd, *waiting[1:3], lo, hi)
+                    added += hi - lo
+                    stores.append((added + PAIR, waiting[0], waiting[2], lo, hi))
+                waiting = None
+            first, own, own_first = 0, list(OWN[s]), 0
+            window = not last_stretch and len(quantised) <= due_behind(s)
+            for g in groups:
+                prepare_to(min(g + LEAD[s], GROUPS - 1))
+                for pair in range(GROUP_TILES[g] // PAIR):
+                    rotate(products, first, g, pair, 0)
+                    if s == 0:
+                        flip_sign()
+                    last_product = window and first + PAIR == count
+                    rotate(products, first, g, pair, 1, 0, 1 if last_product else PAIR)
+                    first += PAIR
+                    if own and first >= own_first + own[0]:
+                        own_last = own_first + own.pop(0)
+                        add(nc.gpsimd, products, qk_out, own_first, own_last)
+                        stores.append((added + own_last + PAIR, groups, qk_out, own_first, own_last))
+                        own_first = own_last
+                    while stores and first >= stores[0][0]:
+                        store_qk(*stores.pop(0)[1:])
+                if not last_product:
                     rotated.append(g)
                     project_what_can_be()
-            if not last_round:
-                first, g, a, c = slots[-1]
-                rotate(products, first, g, a, c, 0, GROUP_TILES[g] - 1)
-            if waiting is not None:
-                for first in range(0, waiting[2], TILES):
-                    store_qk(waiting[0], waiting[1], first, min(first + TILES, waiting[2]))
-            for g in to_transpose[:1]:
-                transpose(g)
-                regroup(g)
-            for region in before:
-                add(nc.vector, products, qk_out, region)
-                if last_round:
-                    store_qk(groups, qk_out, region[2], region[3])
-            for g in ahead[r]:
-                quantise(g)
-                quantised.append(g)
-            for first, g, a, c in slots[-late:]:
-                rotate(products, first, g, a, c, 0 if last_round else GROUP_TILES[g] - 1)
-            rotated.append(g)
-            project_what_can_be()
-            for g in to_transpose[1:]:
-                transpose(g)
-                regroup(g)
-            if not last_round:
-                for region in after:
-                    add(nc.gpsimd, products, qk_out, region)
-                waiting = (groups, qk_out, count)
+            for store in stores:
+                store_qk(*store[1:])
+            if not last_stretch:
+                v_last = own_first + VECTOR[s]
+                quantise_to(due_behind(s))
+                if VECTOR[s]:
+                    add(nc.vector, products, qk_out, own_first, v_last)
+                    store_qk(groups, qk_out, own_first, v_last)
+                if last_product:
+                    rotate(products, count - PAIR, g, GROUP_TILES[g] // PAIR - 1, 1, 1, PAIR)
+                    rotated.append(g)
+                project_what_can_be()
+                if v_last < count:
+                    waiting = (groups, products, qk_out, v_last, count)
             else:
-                for region in after:
-                    add(nc.vector, products, qk_out, region)
-                    store_qk(groups, qk_out, region[2], region[3])
+                for lo in range(own_first, count, PAIR):
+                    add(nc.vector, products, qk_out, lo, lo + PAIR)
+                    store_qk(groups, qk_out, lo, lo + PAIR)

@@ -36,6 +36,7 @@ PREPARED = 6
 BATCH_TILES = 16
 LOADED_AHEAD = 8
 
+WARM0 = 4
 FLOPS = 2 * BATCH * SEQ * HID * (QK + V)
 
 
@@ -95,6 +96,20 @@ def tile_attention_pa_t_kernel(
         nc.sync.dma_start(out=tables[:, 1, :, :], in_=sin.rearrange("(p j) d -> p j d", j=ROWS))
         for g in range(3, LOADED_AHEAD):
             load(g)
+
+        zeros = consts.tile([P, 2 * QK], BF16)
+        nc.vector.memset(zeros[:], 0.0)
+
+        def keep_warm(n):
+            idle_bank = qk_psum.tile([P, PAIR, QK], F32, name="qk_bank")
+            for turn in range(n):
+                nc.tensor.matmul(
+                    out=idle_bank[:].rearrange("p t w -> p (t w)"),
+                    lhsT=zeros[:, 0:P],
+                    rhs=zeros[:],
+                    start=True,
+                    stop=True,
+                )
 
         def transpose(g):
             x_words = x_tiles[g][:].bitcast(F32)
@@ -234,7 +249,11 @@ def tile_attention_pa_t_kernel(
         def due_behind(s):
             return STRETCHES[s + 2][0] if s + 2 < len(STRETCHES) else GROUPS - 1
 
+        keep_warm(WARM0)
+        prepare_to(0)
+        keep_warm(1)
         prepare_to(1)
+        keep_warm(1)
         quantise_to(0)
         project_what_can_be()
         prepare_to(2)

@@ -32,9 +32,10 @@ OWN = [[], [], [], [], [], [2], [], [4], [4], [2]]
 VECTOR = [1, 1, 1, 0, 0, 0, 0, 1, 1, 0]
 
 QK_BANKS = 4
-PREPARED = 6
+PREPARED = 5
 BATCH_TILES = 16
-LOADED_AHEAD = 8
+X_BUFS = 10
+LOADED_AHEAD = 10
 
 WARM0 = 4
 FLOPS = 2 * BATCH * SEQ * HID * (QK + V)
@@ -51,11 +52,10 @@ def tile_attention_pa_t_kernel(
 
     with ExitStack() as stack:
         consts = stack.enter_context(tc.tile_pool(name="consts", bufs=1))
-        x_pool = stack.enter_context(tc.tile_pool(name="x", bufs=LOADED_AHEAD))
+        x_pool = stack.enter_context(tc.tile_pool(name="x", bufs=X_BUFS))
         grouped_pool = stack.enter_context(tc.tile_pool(name="grouped", bufs=PREPARED))
         mx_pool = stack.enter_context(tc.tile_pool(name="mx", bufs=7))
         product_pool = stack.enter_context(tc.tile_pool(name="products", bufs=2))
-        qk_pool = stack.enter_context(tc.tile_pool(name="qk", bufs=4))
         v_pool = stack.enter_context(tc.tile_pool(name="v", bufs=8))
         xt_psum = stack.enter_context(tc.psum_pool(name="xt", bufs=2))
         qk_psum = stack.enter_context(tc.psum_pool(name="qk_sums", bufs=QK_BANKS))
@@ -71,7 +71,10 @@ def tile_attention_pa_t_kernel(
 
         def load(g):
             b, j0, n = where(g)
-            x_tile = x_pool.tile([P, n, HID], BF16)
+            if n == TILES:
+                x_tile = x_pool.tile([P, n, HID], BF16)
+            else:
+                x_tile = x_pool.tile([P, n, HID], BF16, name="x_short")
             nc.sync.dma_start(out=x_tile[:], in_=x_hbm[b, :, j0 : j0 + n, :])
             x_tiles[g] = x_tile
 
@@ -81,6 +84,7 @@ def tile_attention_pa_t_kernel(
         w_words = consts.tile([P, 2 * (QK + V)], U8, align_bytes=64)
         w_scales = consts.tile([P, QK + V], U8, align_bytes=64)
         nc.vector.memset(w_scales[:].bitcast(I32), 0)
+        qk_sums = consts.tile([P, 2, BATCH * ROWS, V], F32)
         tables = consts.tile([P, 2, ROWS, HEAD], BF16)
 
         load(0)
@@ -264,7 +268,8 @@ def tile_attention_pa_t_kernel(
             last_stretch = s + 1 == len(STRETCHES)
             count = tiles_of(groups)
             products = product_pool.tile([P, 2, count, QK], F32)
-            qk_out = qk_pool.tile([P, 2, count, V], F32)
+            start = tiles_of(range(groups[0]))
+            qk_out = qk_sums[:, :, start : start + count, :]
             stores, added = [], 0
             if waiting is not None:
                 for hi in range(waiting[4], waiting[3], -BATCH_TILES):

@@ -28,8 +28,9 @@ GROUPS = len(GROUP_TILES)
 
 STRETCHES = [[0], [1], [2], [3], [4], [5, 6], [7, 8], [9, 10, 11], [12, 13, 14], [15, 16, 17]]
 LEAD = [3, 3, 3, 4, 4, 4, 4, 4, 4, 4]
-OWN = [[], [], [], [], [], [2], [], [4], [4], [2]]
-VECTOR = [1, 1, 1, 0, 0, 0, 0, 1, 1, 0]
+OWN = [[], [], [], [], [], [2], [], [4], [4], [4]]
+TENSOR = [0, 0, 0, 0, 0, 0, 1, 2, 2, 0]
+VECTOR = [1, 1, 1, 0, 0, 0, 0, 0, 1, 0]
 
 QK_BANKS = 4
 PREPARED = 5
@@ -203,6 +204,21 @@ def tile_attention_pa_t_kernel(
                 op=ADD,
             )
 
+        def add_on_tensor(products, qk_out, lo, hi):
+            sums = xt_psum.tile([P, PAIR, 2, P], F32, name="x_transposed")
+            for t in range(hi - lo):
+                for c in range(2):
+                    nc.tensor.matmul(
+                        out=sums[:, t, :, :].rearrange("p a w -> p (a w)"),
+                        lhsT=identity[:],
+                        rhs=products[:, c, lo + t, :],
+                        start=(c == 0),
+                        stop=(c == 1),
+                    )
+            nc.scalar.copy(
+                out=qk_out[:, :, lo:hi, :].rearrange("p a t w -> p t a w"), in_=sums[:, 0 : hi - lo, :, :]
+            )
+
         def store_qk(groups, qk_out, first, last):
             start = sum(GROUP_TILES[: groups[0]])
             while first < last:
@@ -302,8 +318,12 @@ def tile_attention_pa_t_kernel(
             for store in stores:
                 store_qk(*store[1:])
             if not last_stretch:
-                v_last = own_first + VECTOR[s]
+                v_last = own_first + TENSOR[s] + VECTOR[s]
                 quantise_to(due_behind(s))
+                if TENSOR[s]:
+                    add_on_tensor(products, qk_out, own_first, own_first + TENSOR[s])
+                    store_qk(groups, qk_out, own_first, own_first + TENSOR[s])
+                    own_first += TENSOR[s]
                 if VECTOR[s]:
                     add(nc.vector, products, qk_out, own_first, v_last)
                     store_qk(groups, qk_out, own_first, v_last)
@@ -314,6 +334,6 @@ def tile_attention_pa_t_kernel(
                 if v_last < count:
                     waiting = (groups, products, qk_out, v_last, count)
             else:
-                for lo in range(own_first, count, PAIR):
-                    add(nc.vector, products, qk_out, lo, lo + PAIR)
-                    store_qk(groups, qk_out, lo, lo + PAIR)
+                for lo, hi in ((own_first, count - 4), (count - 4, count - 2), (count - 2, count)):
+                    add(nc.vector, products, qk_out, lo, hi)
+                    store_qk(groups, qk_out, lo, hi)

@@ -27,10 +27,15 @@ GROUP_TILES = [2, 2, 2, 2] + [TILES] * (BATCH * ROWS // TILES - 2)
 GROUPS = len(GROUP_TILES)
 
 STRETCHES = [[0], [1], [2], [3], [4], [5, 6], [7, 8], [9, 10, 11], [12, 13, 14], [15, 16, 17]]
-LEAD = [3, 3, 3, 4, 4, 4, 4, 4, 4, 4]
-OWN = [[], [], [], [], [], [2], [], [4], [4], [4]]
-TENSOR = [0, 0, 0, 0, 0, 0, 1, 2, 2, 0]
-VECTOR = [1, 1, 1, 0, 0, 0, 0, 0, 1, 0]
+LEAD = [4, 4, 4, 4, 4, 4, 4, 4, 4, 4]
+MX_BUFS = 6
+OWN = [[], [], [], [], [], [], [], [4], [4], [4]]
+SLOT_T = {16: 2}
+SOFF = 0
+SOFF2 = 2
+TLAG = 2
+TENSOR = [0, 0, 0, 0, 0, 0, 0, 2, 2, 0]
+VECTOR = [2, 2, 2, 0, 0, 1, 1, 0, 2, 0]
 
 QK_BANKS = 4
 PREPARED = 5
@@ -55,7 +60,7 @@ def tile_attention_pa_t_kernel(
         consts = stack.enter_context(tc.tile_pool(name="consts", bufs=1))
         x_pool = stack.enter_context(tc.tile_pool(name="x", bufs=X_BUFS))
         grouped_pool = stack.enter_context(tc.tile_pool(name="grouped", bufs=PREPARED))
-        mx_pool = stack.enter_context(tc.tile_pool(name="mx", bufs=7))
+        mx_pool = stack.enter_context(tc.tile_pool(name="mx", bufs=MX_BUFS))
         product_pool = stack.enter_context(tc.tile_pool(name="products", bufs=2))
         v_pool = stack.enter_context(tc.tile_pool(name="v", bufs=8))
         xt_psum = stack.enter_context(tc.psum_pool(name="xt", bufs=2))
@@ -292,10 +297,14 @@ def tile_attention_pa_t_kernel(
                     lo = max(hi - BATCH_TILES, waiting[3])
                     add(nc.gpsimd, *waiting[1:3], lo, hi)
                     added += hi - lo
-                    stores.append((added + PAIR, waiting[0], waiting[2], lo, hi))
+                    stores.append((added + SOFF, waiting[0], waiting[2], lo, hi))
                 waiting = None
             first, own, own_first = 0, list(OWN[s]), 0
-            window = not last_stretch and len(quantised) <= due_behind(s)
+            window = (
+                not last_stretch
+                and len(quantised) <= due_behind(s)
+                and sum(own) + TENSOR[s] + VECTOR[s] < count
+            )
             for g in groups:
                 prepare_to(min(g + LEAD[s], GROUPS - 1))
                 for pair in range(GROUP_TILES[g] // PAIR):
@@ -308,13 +317,19 @@ def tile_attention_pa_t_kernel(
                     if own and first >= own_first + own[0]:
                         own_last = own_first + own.pop(0)
                         add(nc.gpsimd, products, qk_out, own_first, own_last)
-                        stores.append((added + own_last + PAIR, groups, qk_out, own_first, own_last))
+                        stores.append((added + own_last + SOFF2, groups, qk_out, own_first, own_last))
                         own_first = own_last
                     while stores and first >= stores[0][0]:
                         store_qk(*stores.pop(0)[1:])
                 if not last_product:
                     rotated.append(g)
                     project_what_can_be()
+                n = SLOT_T.get(g, 0)
+                if n:
+                    add_on_tensor(products, qk_out, own_first, own_first + n)
+                    late = (groups, qk_out, own_first, own_first + n)
+                    own_first += n
+                    stores.append((first + TLAG, *late))
             for store in stores:
                 store_qk(*store[1:])
             if not last_stretch:
@@ -334,6 +349,7 @@ def tile_attention_pa_t_kernel(
                 if v_last < count:
                     waiting = (groups, products, qk_out, v_last, count)
             else:
-                for lo, hi in ((own_first, count - 4), (count - 4, count - 2), (count - 2, count)):
+                pieces = ((own_first, count - 4), (count - 4, count - 2), (count - 2, count))
+                for lo, hi in pieces[own_first == count - 4 :]:
                     add(nc.vector, products, qk_out, lo, hi)
                     store_qk(groups, qk_out, lo, hi)

@@ -27,15 +27,15 @@ GROUP_TILES = [2, 2, 2, 2] + [TILES] * (BATCH * ROWS // TILES - 2)
 GROUPS = len(GROUP_TILES)
 
 STRETCHES = [[0], [1], [2], [3], [4], [5, 6], [7, 8], [9, 10, 11], [12, 13, 14], [15, 16, 17]]
-LEAD = [4, 4, 4, 4, 4, 4, 4, 4, 4, 4]
+LEAD = [4, 4, 4, 4, 4, 5, 5, 5, 4, 4]
 MX_BUFS = 6
-OWN = [[], [], [], [], [], [], [], [4], [4], [4]]
+OWN = [[], [], [], [], [], [2], [2], [4], [4], [4]]
 SLOT_T = {16: 2}
 SOFF = 0
 SOFF2 = 2
 TLAG = 2
 TENSOR = [0, 0, 0, 0, 0, 0, 0, 2, 2, 0]
-VECTOR = [2, 2, 2, 0, 0, 1, 1, 0, 2, 0]
+VECTOR = [2, 2, 2, 0, 0, 2, 0, 0, 2, 0]
 
 QK_BANKS = 4
 PREPARED = 5
@@ -43,6 +43,10 @@ BATCH_TILES = 16
 X_BUFS = 10
 LOADED_AHEAD = 10
 
+QK_EDGES = [0, 4, 8, 12, 16, 20, 24, 28, 32, 36, 40, 44, 48, 52, 56, 60, 62, 64]
+
+LATEV = 10
+VLAG = 2
 WARM0 = 4
 FLOPS = 2 * BATCH * SEQ * HID * (QK + V)
 
@@ -201,11 +205,11 @@ def tile_attention_pa_t_kernel(
                 op=MULT,
             )
 
-        def add(engine, products, qk_out, first, last):
+        def add(engine, products, qk_out, first, last, heads=slice(0, 2)):
             engine.tensor_tensor(
-                out=qk_out[:, :, first:last, :].rearrange("p a t w -> p t a w"),
-                in0=products[:, 0, first:last, :].rearrange("p t (a w) -> p t a w", a=2),
-                in1=products[:, 1, first:last, :].rearrange("p t (a w) -> p t a w", a=2),
+                out=qk_out[:, heads, first:last, :].rearrange("p a t w -> p t a w"),
+                in0=products[:, 0, first:last, :].rearrange("p t (a w) -> p t a w", a=2)[:, :, heads, :],
+                in1=products[:, 1, first:last, :].rearrange("p t (a w) -> p t a w", a=2)[:, :, heads, :],
                 op=ADD,
             )
 
@@ -224,16 +228,18 @@ def tile_attention_pa_t_kernel(
                 out=qk_out[:, :, lo:hi, :].rearrange("p a t w -> p t a w"), in_=sums[:, 0 : hi - lo, :, :]
             )
 
+        summed, stored = set(), set()
+
         def store_qk(groups, qk_out, first, last):
-            start = sum(GROUP_TILES[: groups[0]])
-            while first < last:
-                b, j0 = (start + first) // ROWS, (start + first) % ROWS
-                n = min(last - first, ROWS - j0)
-                for a, hbm in enumerate((q_hbm, k_hbm)):
-                    nc.sync.dma_start(
-                        out=hbm[b, :, j0 : j0 + n, :], in_=qk_out[:, a, first : first + n, :]
-                    )
-                first += n
+            start = tiles_of(range(groups[0]))
+            for tile in range(start + first, start + last):
+                summed.add(tile)
+            for lo, hi in zip(QK_EDGES, QK_EDGES[1:]):
+                if lo not in stored and all(tile in summed for tile in range(lo, hi)):
+                    stored.add(lo)
+                    rows = slice(lo % ROWS, lo % ROWS + hi - lo)
+                    for a, hbm in enumerate((q_hbm, k_hbm)):
+                        nc.sync.dma_start(out=hbm[lo // ROWS, :, rows, :], in_=qk_sums[:, a, lo:hi, :])
 
         rotated, quantised, projected, transposed = [], [], [], []
 
@@ -319,6 +325,10 @@ def tile_attention_pa_t_kernel(
                         add(nc.gpsimd, products, qk_out, own_first, own_last)
                         stores.append((added + own_last + SOFF2, groups, qk_out, own_first, own_last))
                         own_first = own_last
+                    if last_stretch and LATEV <= first and own_first < first - VLAG:
+                        add(nc.vector, products, qk_out, own_first, first - VLAG)
+                        stores.append((0, groups, qk_out, own_first, first - VLAG))
+                        own_first = first - VLAG
                     while stores and first >= stores[0][0]:
                         store_qk(*stores.pop(0)[1:])
                 if not last_product:
@@ -349,7 +359,6 @@ def tile_attention_pa_t_kernel(
                 if v_last < count:
                     waiting = (groups, products, qk_out, v_last, count)
             else:
-                pieces = ((own_first, count - 4), (count - 4, count - 2), (count - 2, count))
-                for lo, hi in pieces[own_first == count - 4 :]:
-                    add(nc.vector, products, qk_out, lo, hi)
-                    store_qk(groups, qk_out, lo, hi)
+                for lo in range(own_first, count, PAIR):
+                    add(nc.vector, products, qk_out, lo, lo + PAIR)
+                    store_qk(groups, qk_out, lo, lo + PAIR)

from contextlib import ExitStack

import concourse.mybir as mybir
from concourse.masks import make_identity

F32 = mybir.dt.float32
BF16 = mybir.dt.bfloat16
I32 = mybir.dt.int32
U32 = mybir.dt.uint32
U8 = mybir.dt.uint8
FP8X4 = mybir.dt.float8_e4m3fn_x4
FP4X4 = mybir.dt.float4_e2m1fn_x4
MULT = mybir.AluOpType.mult
ADD = mybir.AluOpType.add

P = 128
BATCH, SEQ, HID = 4, 2048, 512
HEAD = 64
HALF = HEAD // 2
QK_HEADS = 4
QK = QK_HEADS * HEAD
V = 2 * HEAD
ROWS = SEQ // P
TILES = 4
PAIR = 2
GROUP_TILES = [2, 2, 2, 2] + [TILES] * (BATCH * ROWS // TILES - 2)
GROUPS = len(GROUP_TILES)

STRETCHES = [[0], [1], [2], [3], [4], [5, 6], [7, 8], [9, 10, 11], [12, 13, 14], [15, 16, 17]]
LEAD = [4, 4, 4, 4, 4, 5, 5, 5, 4, 4]
MX_BUFS = 6
OWN = [[], [], [], [], [], [2], [2], [4], [4], [4]]
SLOT_T = {16: 2}
SOFF = 0
SOFF2 = 2
TLAG = 2
TENSOR = [0, 0, 0, 0, 0, 0, 0, 2, 2, 0]
VECTOR = [2, 2, 2, 0, 0, 2, 0, 0, 2, 0]

QK_BANKS = 4
PREPARED = 5
BATCH_TILES = 16
X_BUFS = 10
LOADED_AHEAD = 10

QK_EDGES = [0, 4, 8, 12, 16, 20, 24, 28, 32, 36, 40, 44, 48, 52, 56, 60, 62, 64]

LATEV = 10
VLAG = 2
WARM0 = 4
FLOPS = 2 * BATCH * SEQ * HID * (QK + V)


def tile_attention_pa_t_kernel(
    tc, hidden_states, cos, sin, w_qkv_words, w_qkv_scales, out_0, out_1, out_2
):
    nc = tc.nc
    x_hbm = hidden_states.rearrange("b (p j) k -> b p j k", j=ROWS)
    q_hbm = out_0.rearrange("b (p j) h d -> b p j (h d)", j=ROWS)
    k_hbm = out_1.rearrange("b (p j) h d -> b p j (h d)", j=ROWS)
    v_hbm = out_2.rearrange("b (p j) h d -> b p j (h d)", j=ROWS)

    with ExitStack() as stack:
        consts = stack.enter_context(tc.tile_pool(name="consts", bufs=1))
        x_pool = stack.enter_context(tc.tile_pool(name="x", bufs=X_BUFS))
        grouped_pool = stack.enter_context(tc.tile_pool(name="grouped", bufs=PREPARED))
        mx_pool = stack.enter_context(tc.tile_pool(name="mx", bufs=MX_BUFS))
        product_pool = stack.enter_context(tc.tile_pool(name="products", bufs=2))
        v_pool = stack.enter_context(tc.tile_pool(name="v", bufs=8))
        xt_psum = stack.enter_context(tc.psum_pool(name="xt", bufs=2))
        qk_psum = stack.enter_context(tc.psum_pool(name="qk_sums", bufs=QK_BANKS))
        v_psum = stack.enter_context(tc.psum_pool(name="v_sums", bufs=2))
        stack.enter_context(tc.manual_schedule())

        x_tiles, xt_tiles, grouped_tiles, code_tiles, scale_tiles = {}, {}, {}, {}, {}
        qk_banks, v_banks = {}, {}

        def where(g):
            first = sum(GROUP_TILES[:g])
            return first // ROWS, first % ROWS, GROUP_TILES[g]

        def load(g):
            b, j0, n = where(g)
            if n == TILES:
                x_tile = x_pool.tile([P, n, HID], BF16)
            else:
                x_tile = x_pool.tile([P, n, HID], BF16, name="x_short")
            nc.sync.dma_start(out=x_tile[:], in_=x_hbm[b, :, j0 : j0 + n, :])
            x_tiles[g] = x_tile

        identity = consts.tile([P, P], F32)
        make_identity(nc, identity[:])

        w_words = consts.tile([P, 2 * (QK + V)], U8, align_bytes=64)
        w_scales = consts.tile([P, QK + V], U8, align_bytes=64)
        nc.vector.memset(w_scales[:].bitcast(I32), 0)
        qk_sums = consts.tile([P, 2, BATCH * ROWS, V], F32)
        tables = consts.tile([P, 2, ROWS, HEAD], BF16)

        load(0)
        nc.sync.dma_start(out=w_words[:].bitcast(I32), in_=w_qkv_words[0].bitcast(I32))
        for quadrant in range(4):
            nc.sync.dma_start(
                out=w_scales[32 * quadrant : 32 * quadrant + 4, :].bitcast(I32),
                in_=w_qkv_scales[0, 4 * quadrant : 4 * quadrant + 4, :].bitcast(I32),
            )
        load(1)
        nc.sync.dma_start(out=tables[:, 0, :, :], in_=cos.rearrange("(p j) d -> p j d", j=ROWS))
        load(2)
        nc.sync.dma_start(out=tables[:, 1, :, :], in_=sin.rearrange("(p j) d -> p j d", j=ROWS))
        for g in range(3, LOADED_AHEAD):
            load(g)

        zeros = consts.tile([P, 2 * QK], BF16)
        nc.vector.memset(zeros[:], 0.0)

        def keep_warm(n):
            idle_bank = qk_psum.tile([P, PAIR, QK], F32, name="qk_bank")
            for turn in range(n):
                nc.tensor.matmul(
                    out=idle_bank[:].rearrange("p t w -> p (t w)"),
                    lhsT=zeros[:, 0:P],
                    rhs=zeros[:],
                    start=True,
                    stop=True,
                )

        def transpose(g):
            x_words = x_tiles[g][:].bitcast(F32)
            xt_tiles[g] = []
            for pair in range(GROUP_TILES[g] // PAIR):
                x_transposed = xt_psum.tile([P, PAIR, 2, P], F32)
                for t in range(PAIR):
                    for u in range(2):
                        nc.tensor.transpose(
                            x_transposed[:, t, u, :],
                            x_words[:, PAIR * pair + t, u : HID // 2 : 2],
                            identity[:],
                        )
                xt_tiles[g].append(x_transposed)

        def regroup(g):
            n = GROUP_TILES[g]
            grouped = grouped_pool.tile([P, n * P * 4], BF16, align_bytes=64)
            grouped_words = grouped[:].bitcast(F32).rearrange("p (t r u) -> p t r u", t=n, u=2)
            for pair in range(n // PAIR):
                nc.scalar.copy(
                    out=grouped_words[:, PAIR * pair : PAIR * (pair + 1), :, :],
                    in_=xt_tiles[g][pair][:].rearrange("p t u r -> p t r u"),
                )
            grouped_tiles[g] = grouped

        def quantise(g):
            codes = mx_pool.tile([P, GROUP_TILES[g] * P], U32, align_bytes=64)
            scales = mx_pool.tile([P, GROUP_TILES[g] * P], U8, align_bytes=64)
            nc.vector.quantize_mx(
                out=codes[:].bitcast(FP8X4), scales=scales[:], in_=grouped_tiles[g][:]
            )
            code_tiles[g], scale_tiles[g] = codes, scales

        def multiply(bank_columns, g, t, first, last):
            tokens = slice(P * t, P * (t + 1))
            nc.tensor.matmul_mx(
                out=bank_columns,
                lhsT=code_tiles[g][:, tokens].bitcast(FP8X4),
                lhsT_scale=scale_tiles[g][:, tokens],
                rhs=w_words[:, 2 * first : 2 * last].bitcast(FP4X4),
                rhs_scale=w_scales[:, first:last],
                start=True,
                stop=True,
            )

        def project(g):
            qk_banks[g] = []
            for pair in range(GROUP_TILES[g] // PAIR):
                qk_bank = qk_psum.tile([P, PAIR, QK], F32)
                for t in range(PAIR):
                    multiply(qk_bank[:, t, :], g, PAIR * pair + t, 0, QK)
                qk_banks[g].append(qk_bank)
            v_bank = v_psum.tile([P, GROUP_TILES[g], V], F32)
            for t in range(GROUP_TILES[g]):
                multiply(v_bank[:, t, :], g, t, QK, QK + V)
            v_banks[g] = v_bank

        def store_v(g):
            b, j0, n = where(g)
            v_out = v_pool.tile([P, n, V], F32)
            nc.scalar.copy(out=v_out[:], in_=v_banks[g][:])
            nc.sync.dma_start(out=v_hbm[b, :, j0 : j0 + n, :], in_=v_out[:])

        def rotate(products, first, g, pair, c, t0=0, t1=PAIR):
            j0, first, n = where(g)[1] + PAIR * pair + t0, first + t0, t1 - t0
            halves = qk_banks[g][pair][:, t0:t1, :].rearrange(
                "p t (g two w) -> p t g two w", two=2, w=HALF
            )
            nc.vector.tensor_tensor(
                out=products[:, c, first : first + n, :].rearrange(
                    "p t (g two w) -> p t g two w", two=2, w=HALF
                ),
                in0=halves if c == 0 else halves[:, :, :, ::-1, :],
                in1=tables[:, c, j0 : j0 + n, :]
                .rearrange("p t (two w) -> p t two w", two=2)
                .unsqueeze(2)
                .to_broadcast([P, n, QK_HEADS, 2, HALF]),
                op=MULT,
            )

        def add(engine, products, qk_out, first, last, heads=slice(0, 2)):
            engine.tensor_tensor(
                out=qk_out[:, heads, first:last, :].rearrange("p a t w -> p t a w"),
                in0=products[:, 0, first:last, :].rearrange("p t (a w) -> p t a w", a=2)[:, :, heads, :],
                in1=products[:, 1, first:last, :].rearrange("p t (a w) -> p t a w", a=2)[:, :, heads, :],
                op=ADD,
            )

        def add_on_tensor(products, qk_out, lo, hi):
            sums = xt_psum.tile([P, PAIR, 2, P], F32, name="x_transposed")
            for t in range(hi - lo):
                for c in range(2):
                    nc.tensor.matmul(
                        out=sums[:, t, :, :].rearrange("p a w -> p (a w)"),
                        lhsT=identity[:],
                        rhs=products[:, c, lo + t, :],
                        start=(c == 0),
                        stop=(c == 1),
                    )
            nc.scalar.copy(
                out=qk_out[:, :, lo:hi, :].rearrange("p a t w -> p t a w"), in_=sums[:, 0 : hi - lo, :, :]
            )

        summed, stored = set(), set()

        def store_qk(groups, qk_out, first, last):
            start = tiles_of(range(groups[0]))
            for tile in range(start + first, start + last):
                summed.add(tile)
            for lo, hi in zip(QK_EDGES, QK_EDGES[1:]):
                if lo not in stored and all(tile in summed for tile in range(lo, hi)):
                    stored.add(lo)
                    rows = slice(lo % ROWS, lo % ROWS + hi - lo)
                    for a, hbm in enumerate((q_hbm, k_hbm)):
                        nc.sync.dma_start(out=hbm[lo // ROWS, :, rows, :], in_=qk_sums[:, a, lo:hi, :])

        rotated, quantised, projected, transposed = [], [], [], []

        def flip_sign():
            nc.vector.tensor_scalar(
                out=tables[:, 1, :, 0:HALF],
                in0=tables[:, 1, :, 0:HALF],
                scalar1=-1.0,
                scalar2=None,
                op0=MULT,
            )

        def tiles_of(groups):
            return sum(GROUP_TILES[g] for g in groups)

        def project_what_can_be():
            while (
                len(projected) < len(quantised)
                and tiles_of(projected + [len(projected)]) - tiles_of(rotated) <= PAIR * QK_BANKS
            ):
                project(len(projected))
                store_v(len(projected))
                projected.append(len(projected))

        def prepare_to(g):
            while len(transposed) <= min(g, GROUPS - 1):
                transpose(len(transposed))
                regroup(len(transposed))
                if len(transposed) + LOADED_AHEAD < GROUPS:
                    load(len(transposed) + LOADED_AHEAD)
                transposed.append(len(transposed))

        def quantise_to(g):
            while len(quantised) <= g:
                quantise(len(quantised))
                quantised.append(len(quantised))

        def due_behind(s):
            return STRETCHES[s + 2][0] if s + 2 < len(STRETCHES) else GROUPS - 1

        keep_warm(WARM0)
        prepare_to(0)
        keep_warm(1)
        prepare_to(1)
        keep_warm(1)
        quantise_to(0)
        project_what_can_be()
        prepare_to(2)
        quantise_to(1)
        project_what_can_be()
        waiting = None
        for s, groups in enumerate(STRETCHES):
            last_stretch = s + 1 == len(STRETCHES)
            count = tiles_of(groups)
            products = product_pool.tile([P, 2, count, QK], F32)
            start = tiles_of(range(groups[0]))
            qk_out = qk_sums[:, :, start : start + count, :]
            stores, added = [], 0
            if waiting is not None:
                for hi in range(waiting[4], waiting[3], -BATCH_TILES):
                    lo = max(hi - BATCH_TILES, waiting[3])
                    add(nc.gpsimd, *waiting[1:3], lo, hi)
                    added += hi - lo
                    stores.append((added + SOFF, waiting[0], waiting[2], lo, hi))
                waiting = None
            first, own, own_first = 0, list(OWN[s]), 0
            window = (
                not last_stretch
                and len(quantised) <= due_behind(s)
                and sum(own) + TENSOR[s] + VECTOR[s] < count
            )
            for g in groups:
                prepare_to(min(g + LEAD[s], GROUPS - 1))
                for pair in range(GROUP_TILES[g] // PAIR):
                    rotate(products, first, g, pair, 0)
                    if s == 0:
                        flip_sign()
                    last_product = window and first + PAIR == count
                    rotate(products, first, g, pair, 1, 0, 1 if last_product else PAIR)
                    first += PAIR
                    if own and first >= own_first + own[0]:
                        own_last = own_first + own.pop(0)
                        add(nc.gpsimd, products, qk_out, own_first, own_last)
                        stores.append((added + own_last + SOFF2, groups, qk_out, own_first, own_last))
                        own_first = own_last
                    if last_stretch and LATEV <= first and own_first < first - VLAG:
                        add(nc.vector, products, qk_out, own_first, first - VLAG)
                        stores.append((0, groups, qk_out, own_first, first - VLAG))
                        own_first = first - VLAG
                    while stores and first >= stores[0][0]:
                        store_qk(*stores.pop(0)[1:])
                if not last_product:
                    rotated.append(g)
                    project_what_can_be()
                n = SLOT_T.get(g, 0)
                if n:
                    add_on_tensor(products, qk_out, own_first, own_first + n)
                    late = (groups, qk_out, own_first, own_first + n)
                    own_first += n
                    stores.append((first + TLAG, *late))
            for store in stores:
                store_qk(*store[1:])
            if not last_stretch:
                v_last = own_first + TENSOR[s] + VECTOR[s]
                quantise_to(due_behind(s))
                if TENSOR[s]:
                    add_on_tensor(products, qk_out, own_first, own_first + TENSOR[s])
                    store_qk(groups, qk_out, own_first, own_first + TENSOR[s])
                    own_first += TENSOR[s]
                if VECTOR[s]:
                    add(nc.vector, products, qk_out, own_first, v_last)
                    store_qk(groups, qk_out, own_first, v_last)
                if last_product:
                    rotate(products, count - PAIR, g, GROUP_TILES[g] // PAIR - 1, 1, 1, PAIR)
                    rotated.append(g)
                project_what_can_be()
                if v_last < count:
                    waiting = (groups, products, qk_out, v_last, count)
            else:
                for lo in range(own_first, count, PAIR):
                    add(nc.vector, products, qk_out, lo, lo + PAIR)
                    store_qk(groups, qk_out, lo, lo + PAIR)
